import numpy as np
import ml_dtypes


def mxq(x, axis, fmt="e4m3"):
    dtype, down = {"e4m3": (ml_dtypes.float8_e4m3fn, 7), "e5m2": (ml_dtypes.float8_e5m2, 14)}[fmt]
    v = np.moveaxis(np.asarray(x, np.float32).astype(ml_dtypes.bfloat16).astype(np.float64), axis, -1)
    blocks = v.reshape(v.shape[:-1] + (-1, 32))
    amax = np.abs(blocks).max(-1, keepdims=True)
    byte = np.maximum(np.where(amax > 0, np.frexp(amax)[1] - 1 + 127, 0) - down, 1)
    scale = np.exp2(byte - 127.0)
    codes = (blocks / scale).astype(np.float32).astype(dtype).astype(np.float64)
    return np.moveaxis((codes * scale).reshape(v.shape), -1, axis)


WIDE = False


def mx_kscale(k):
    if not WIDE:
        return np.ones(k)
    levels = np.array([10, -10, 5, -5, 0])
    a = np.random.permutation(np.resize(levels, k // 512 * 4)).reshape(k // 512, 4)
    idx = np.arange(k)
    return np.exp2(a[idx // 512, idx % 128 // 32])


BF16 = ml_dtypes.bfloat16


def bf(x):
    return np.asarray(x, np.float32).astype(BF16)


def f64(x):
    return np.asarray(x).astype(np.float64)


N, C, H, W, B = 512, 128, 4, 4, 128
D = C * H * W


def setup_inputs():
    s = mx_kscale(N)
    sig = (0.5 + 0.5 * np.random.random((B, 1))) * (1.0 + np.random.random((B, 1)))
    z = np.random.standard_normal((B, N)) * sig
    e = np.exp(z - z.max(1, keepdims=True))
    w = e / e.sum(1, keepdims=True)
    memory = np.random.standard_normal((N, D)) * (0.5 + np.random.random((N, 1))) * 3.0
    add = np.random.standard_normal((B, C, H, W)) * 3.0 * np.sqrt(N / B)
    return {"w": bf(w * s), "memory": bf((memory / s[:, None]).reshape(N, C, H, W)), "add": bf(add / np.mean(s * s))}


def reference(w, memory, add):
    wf = f64(w)
    mem_flat = f64(memory).reshape(N, D)
    a = f64(add).reshape(B, D)
    new_memory = mem_flat + wf.T @ a
    r = mxq(wf, 1, "e4m3") @ mxq(new_memory, 0, "e4m3")
    return r.reshape(B, C, H, W)

@@ -1,0 +1,108 @@
+from contextlib import ExitStack
+
+import concourse.mybir as mybir
+from concourse.masks import make_identity
+
+BF16 = mybir.dt.bfloat16
+F32 = mybir.dt.float32
+U32 = mybir.dt.uint32
+U8 = mybir.dt.uint8
+FP8X4 = mybir.dt.float8_e4m3fn_x4
+
+P = 128
+PACK = 4
+SLOTS = P * PACK
+WIDTH = 2048
+BANK_COLS = 128
+PASS_COLS = 512
+N_PASSES = WIDTH // PASS_COLS
+BANKS_PER_PASS = PASS_COLS // BANK_COLS
+
+FLOPS = 2 * (2 * P * SLOTS * WIDTH)
+
+
+def tile_memory_pb_s_kernel(tc, w, memory, add, out):
+    nc = tc.nc
+    mem_rows = memory.rearrange("(p t) c h w -> p t (c h w)", t=PACK)
+    add_rows = add.rearrange("b c h w -> b (c h w)")
+    out_rows = out.rearrange("b c h w -> b (c h w)")
+
+    with ExitStack() as ctx:
+        keep = ctx.enter_context(tc.tile_pool(name="keep", bufs=1))
+        loads = ctx.enter_context(tc.tile_pool(name="loads", bufs=N_PASSES))
+        work = ctx.enter_context(tc.tile_pool(name="work", bufs=2))
+        psum_w = ctx.enter_context(tc.psum_pool(name="psum_w", bufs=1))
+        psum_new = ctx.enter_context(tc.psum_pool(name="psum_new", bufs=5))
+        psum_out = ctx.enter_context(tc.psum_pool(name="psum_out", bufs=2))
+
+        w_sb = keep.tile([P, SLOTS], BF16)
+        nc.sync.dma_start(out=w_sb[:], in_=w)
+        a_tiles = []
+        mem_tiles = []
+        for c in range(N_PASSES):
+            cols = slice(c * PASS_COLS, (c + 1) * PASS_COLS)
+            a_sb = loads.tile([P, PASS_COLS], BF16)
+            nc.sync.dma_start(out=a_sb[:], in_=add_rows[:, cols])
+            mem_sb = loads.tile([P, PACK, PASS_COLS], BF16)
+            nc.sync.dma_start(out=mem_sb[:], in_=mem_rows[:, :, cols])
+            a_tiles.append(a_sb)
+            mem_tiles.append(mem_sb)
+
+        ident = keep.tile([P, P], BF16)
+        make_identity(nc, ident[:])
+
+        w_by_t = keep.tile([P, PACK, P], BF16)
+        nc.vector.tensor_copy(out=w_by_t[:], in_=w_sb[:].rearrange("b (p t) -> b t p", t=PACK))
+
+        wT_ps = psum_w.tile([P, PACK, P], BF16)
+        for t in range(PACK):
+            nc.tensor.transpose(wT_ps[:, t, :], w_by_t[:, t, :], ident[:])
+        w_grouped = keep.tile([P, P, PACK], BF16, align_bytes=64)
+        nc.scalar.copy(out=w_grouped[:], in_=wT_ps[:].rearrange("p t b -> p b t"))
+        w_codes = keep.tile([P, P], U32, align_bytes=64)
+        w_scales = keep.tile([P, P], U8, align_bytes=64)
+        nc.vector.quantize_mx(
+            out=w_codes[:].bitcast(FP8X4),
+            scales=w_scales[:],
+            in_=w_grouped[:].rearrange("p b t -> p (b t)"),
+        )
+
+        for c in range(N_PASSES):
+            new_grouped = work.tile([P, PASS_COLS, PACK], BF16, align_bytes=64)
+            for j in range(BANKS_PER_PASS):
+                cols = slice(j * BANK_COLS, (j + 1) * BANK_COLS)
+                written = psum_new.tile([P, PACK, BANK_COLS], F32)
+                for t in range(PACK):
+                    nc.tensor.matmul(
+                        written[:, t, :],
+                        lhsT=w_by_t[:, t, :],
+                        rhs=a_tiles[c][:, cols],
+                        start=True,
+                        stop=True,
+                    )
+                nc.vector.tensor_tensor(
+                    out=new_grouped[:, cols, :],
+                    in0=written[:].rearrange("p t d -> p d t"),
+                    in1=mem_tiles[c][:, :, cols].rearrange("p t d -> p d t"),
+                    op=mybir.AluOpType.add,
+                )
+            new_codes = work.tile([P, PASS_COLS], U32, align_bytes=64)
+            new_scales = work.tile([P, PASS_COLS], U8, align_bytes=64)
+            nc.vector.quantize_mx(
+                out=new_codes[:].bitcast(FP8X4),
+                scales=new_scales[:],
+                in_=new_grouped[:].rearrange("p d t -> p (d t)"),
+            )
+            read = psum_out.tile([P, PASS_COLS], F32)
+            nc.tensor.matmul_mx(
+                out=read[:],
+                lhsT=w_codes[:].bitcast(FP8X4),
+                lhsT_scale=w_scales[:],
+                rhs=new_codes[:].bitcast(FP8X4),
+                rhs_scale=new_scales[:],
+                start=True,
+                stop=True,
+            )
+            result = work.tile([P, PASS_COLS], F32)
+            nc.scalar.copy(out=result[:], in_=read[:])
+            nc.sync.dma_start(out=out_rows[:, c * PASS_COLS : (c + 1) * PASS_COLS], in_=result[:])

@@ -14,9 +14,12 @@ PACK = 4
 SLOTS = P * PACK
 WIDTH = 2048
 BANK_COLS = 128
-PASS_COLS = 512
-N_PASSES = WIDTH // PASS_COLS
-BANKS_PER_PASS = PASS_COLS // BANK_COLS
+PIECE_COLS = 256
+N_PIECES = WIDTH // PIECE_COLS
+BANKS_PER_PIECE = PIECE_COLS // BANK_COLS
+N_BANKS = WIDTH // BANK_COLS
+NEW_BANKS = 5
+LEAD = NEW_BANKS - 1
 
 FLOPS = 2 * (2 * P * SLOTS * WIDTH)
 
@@ -28,22 +31,23 @@ def tile_memory_pb_s_kernel(tc, w, memory, add, out):
     out_rows = out.rearrange("b c h w -> b (c h w)")
 
     with ExitStack() as ctx:
+        ctx.enter_context(tc.manual_schedule())
         keep = ctx.enter_context(tc.tile_pool(name="keep", bufs=1))
-        loads = ctx.enter_context(tc.tile_pool(name="loads", bufs=N_PASSES))
-        work = ctx.enter_context(tc.tile_pool(name="work", bufs=2))
+        pieces = ctx.enter_context(tc.tile_pool(name="pieces", bufs=N_PIECES))
+        work = ctx.enter_context(tc.tile_pool(name="work", bufs=3))
         psum_w = ctx.enter_context(tc.psum_pool(name="psum_w", bufs=1))
-        psum_new = ctx.enter_context(tc.psum_pool(name="psum_new", bufs=5))
+        psum_new = ctx.enter_context(tc.psum_pool(name="psum_new", bufs=NEW_BANKS))
         psum_out = ctx.enter_context(tc.psum_pool(name="psum_out", bufs=2))
 
         w_sb = keep.tile([P, SLOTS], BF16)
         nc.sync.dma_start(out=w_sb[:], in_=w)
         a_tiles = []
         mem_tiles = []
-        for c in range(N_PASSES):
-            cols = slice(c * PASS_COLS, (c + 1) * PASS_COLS)
-            a_sb = loads.tile([P, PASS_COLS], BF16)
+        for i in range(N_PIECES):
+            cols = slice(i * PIECE_COLS, (i + 1) * PIECE_COLS)
+            a_sb = pieces.tile([P, PIECE_COLS], BF16)
             nc.sync.dma_start(out=a_sb[:], in_=add_rows[:, cols])
-            mem_sb = loads.tile([P, PACK, PASS_COLS], BF16)
+            mem_sb = pieces.tile([P, PACK, PIECE_COLS], BF16)
             nc.sync.dma_start(out=mem_sb[:], in_=mem_rows[:, :, cols])
             a_tiles.append(a_sb)
             mem_tiles.append(mem_sb)
@@ -54,46 +58,61 @@ def tile_memory_pb_s_kernel(tc, w, memory, add, out):
         w_by_t = keep.tile([P, PACK, P], BF16)
         nc.vector.tensor_copy(out=w_by_t[:], in_=w_sb[:].rearrange("b (p t) -> b t p", t=PACK))
 
-        wT_ps = psum_w.tile([P, PACK, P], BF16)
-        for t in range(PACK):
-            nc.tensor.transpose(wT_ps[:, t, :], w_by_t[:, t, :], ident[:])
         w_grouped = keep.tile([P, P, PACK], BF16, align_bytes=64)
-        nc.scalar.copy(out=w_grouped[:], in_=wT_ps[:].rearrange("p t b -> p b t"))
         w_codes = keep.tile([P, P], U32, align_bytes=64)
         w_scales = keep.tile([P, P], U8, align_bytes=64)
-        nc.vector.quantize_mx(
-            out=w_codes[:].bitcast(FP8X4),
-            scales=w_scales[:],
-            in_=w_grouped[:].rearrange("p b t -> p (b t)"),
-        )
 
-        for c in range(N_PASSES):
-            new_grouped = work.tile([P, PASS_COLS, PACK], BF16, align_bytes=64)
-            for j in range(BANKS_PER_PASS):
-                cols = slice(j * BANK_COLS, (j + 1) * BANK_COLS)
-                written = psum_new.tile([P, PACK, BANK_COLS], F32)
-                for t in range(PACK):
-                    nc.tensor.matmul(
-                        written[:, t, :],
-                        lhsT=w_by_t[:, t, :],
-                        rhs=a_tiles[c][:, cols],
-                        start=True,
-                        stop=True,
-                    )
-                nc.vector.tensor_tensor(
-                    out=new_grouped[:, cols, :],
-                    in0=written[:].rearrange("p t d -> p d t"),
-                    in1=mem_tiles[c][:, :, cols].rearrange("p t d -> p d t"),
-                    op=mybir.AluOpType.add,
+        def transpose_w():
+            wT_ps = psum_w.tile([P, PACK, P], BF16)
+            for t in range(PACK):
+                nc.tensor.transpose(wT_ps[:, t, :], w_by_t[:, t, :], ident[:])
+            nc.scalar.copy(out=w_grouped[:], in_=wT_ps[:].rearrange("p t b -> p b t"))
+
+        def quantise_w():
+            nc.vector.quantize_mx(
+                out=w_codes[:].bitcast(FP8X4),
+                scales=w_scales[:],
+                in_=w_grouped[:].rearrange("p b t -> p (b t)"),
+            )
+
+        written_banks = {}
+        grouped_tiles = {}
+
+        def write_bank(u):
+            i, j = divmod(u, BANKS_PER_PIECE)
+            written = psum_new.tile([P, PACK, BANK_COLS], F32)
+            for t in range(PACK):
+                nc.tensor.matmul(
+                    written[:, t, :],
+                    lhsT=w_by_t[:, t, :],
+                    rhs=a_tiles[i][:, j * BANK_COLS : (j + 1) * BANK_COLS],
+                    start=True,
+                    stop=True,
                 )
-            new_codes = work.tile([P, PASS_COLS], U32, align_bytes=64)
-            new_scales = work.tile([P, PASS_COLS], U8, align_bytes=64)
+            written_banks[u] = written
+
+        def add_bank(u):
+            i, j = divmod(u, BANKS_PER_PIECE)
+            if j == 0:
+                new_grouped = work.tile([P, PIECE_COLS, PACK], BF16, align_bytes=64)
+                grouped_tiles[i] = new_grouped
+            cols = slice(j * BANK_COLS, (j + 1) * BANK_COLS)
+            nc.vector.tensor_tensor(
+                out=grouped_tiles[i][:, cols, :],
+                in0=written_banks[u][:].rearrange("p t d -> p d t"),
+                in1=mem_tiles[i][:, :, cols].rearrange("p t d -> p d t"),
+                op=mybir.AluOpType.add,
+            )
+
+        def read_piece(i):
+            new_codes = work.tile([P, PIECE_COLS], U32, align_bytes=64)
+            new_scales = work.tile([P, PIECE_COLS], U8, align_bytes=64)
             nc.vector.quantize_mx(
                 out=new_codes[:].bitcast(FP8X4),
                 scales=new_scales[:],
-                in_=new_grouped[:].rearrange("p d t -> p (d t)"),
+                in_=grouped_tiles[i][:].rearrange("p d t -> p (d t)"),
             )
-            read = psum_out.tile([P, PASS_COLS], F32)
+            read = psum_out.tile([P, PIECE_COLS], F32)
             nc.tensor.matmul_mx(
                 out=read[:],
                 lhsT=w_codes[:].bitcast(FP8X4),
@@ -103,6 +122,20 @@ def tile_memory_pb_s_kernel(tc, w, memory, add, out):
                 start=True,
                 stop=True,
             )
-            result = work.tile([P, PASS_COLS], F32)
+            result = pieces.tile([P, PIECE_COLS], F32)
             nc.scalar.copy(out=result[:], in_=read[:])
-            nc.sync.dma_start(out=out_rows[:, c * PASS_COLS : (c + 1) * PASS_COLS], in_=result[:])
+            nc.sync.dma_start(out=out_rows[:, i * PIECE_COLS : (i + 1) * PIECE_COLS], in_=result[:])
+
+        for u in range(LEAD):
+            write_bank(u)
+            if u == BANKS_PER_PIECE - 1:
+                transpose_w()
+        for u in range(N_BANKS):
+            if u + LEAD < N_BANKS:
+                write_bank(u + LEAD)
+            add_bank(u)
+            if u == BANKS_PER_PIECE:
+                quantise_w()
+            if u >= BANKS_PER_PIECE and u % BANKS_PER_PIECE == 0:
+                read_piece(u // BANKS_PER_PIECE - 1)
+        read_piece(N_PIECES - 1)

@@ -20,6 +20,7 @@ BANKS_PER_PIECE = PIECE_COLS // BANK_COLS
 N_BANKS = WIDTH // BANK_COLS
 NEW_BANKS = 5
 LEAD = NEW_BANKS - 1
+SHARE = 4
 
 FLOPS = 2 * (2 * P * SLOTS * WIDTH)
 
@@ -34,7 +35,7 @@ def tile_memory_pb_s_kernel(tc, w, memory, add, out):
         ctx.enter_context(tc.manual_schedule())
         keep = ctx.enter_context(tc.tile_pool(name="keep", bufs=1))
         pieces = ctx.enter_context(tc.tile_pool(name="pieces", bufs=N_PIECES))
-        work = ctx.enter_context(tc.tile_pool(name="work", bufs=3))
+        stage = ctx.enter_context(tc.tile_pool(name="stage", bufs=N_BANKS // SHARE))
         psum_w = ctx.enter_context(tc.psum_pool(name="psum_w", bufs=1))
         psum_new = ctx.enter_context(tc.psum_pool(name="psum_new", bufs=NEW_BANKS))
         psum_out = ctx.enter_context(tc.psum_pool(name="psum_out", bufs=2))
@@ -68,15 +69,11 @@ def tile_memory_pb_s_kernel(tc, w, memory, add, out):
                 nc.tensor.transpose(wT_ps[:, t, :], w_by_t[:, t, :], ident[:])
             nc.scalar.copy(out=w_grouped[:], in_=wT_ps[:].rearrange("p t b -> p b t"))
 
-        def quantise_w():
-            nc.vector.quantize_mx(
-                out=w_codes[:].bitcast(FP8X4),
-                scales=w_scales[:],
-                in_=w_grouped[:].rearrange("p b t -> p (b t)"),
-            )
-
         written_banks = {}
-        grouped_tiles = {}
+        grouped_tiles = []
+        for i in range(N_PIECES):
+            new_grouped = pieces.tile([P, PIECE_COLS, PACK], BF16, align_bytes=64)
+            grouped_tiles.append(new_grouped)
 
         def write_bank(u):
             i, j = divmod(u, BANKS_PER_PIECE)
@@ -93,20 +90,23 @@ def tile_memory_pb_s_kernel(tc, w, memory, add, out):
 
         def add_bank(u):
             i, j = divmod(u, BANKS_PER_PIECE)
-            if j == 0:
-                new_grouped = work.tile([P, PIECE_COLS, PACK], BF16, align_bytes=64)
-                grouped_tiles[i] = new_grouped
             cols = slice(j * BANK_COLS, (j + 1) * BANK_COLS)
-            nc.vector.tensor_tensor(
-                out=grouped_tiles[i][:, cols, :],
-                in0=written_banks[u][:].rearrange("p t d -> p d t"),
-                in1=mem_tiles[i][:, :, cols].rearrange("p t d -> p d t"),
-                op=mybir.AluOpType.add,
-            )
+            written_by_col = written_banks[u][:].rearrange("p t d -> p d t")
+            mem_by_col = mem_tiles[i][:, :, cols].rearrange("p t d -> p d t")
+            if u % SHARE == 1:
+                staged = stage.tile([P, BANK_COLS, PACK], F32)
+                nc.scalar.copy(out=staged[:], in_=written_by_col)
+                nc.gpsimd.tensor_tensor(
+                    out=grouped_tiles[i][:, cols, :], in0=staged[:], in1=mem_by_col, op=mybir.AluOpType.add
+                )
+            else:
+                nc.vector.tensor_tensor(
+                    out=grouped_tiles[i][:, cols, :], in0=written_by_col, in1=mem_by_col, op=mybir.AluOpType.add
+                )
 
         def read_piece(i):
-            new_codes = work.tile([P, PIECE_COLS], U32, align_bytes=64)
-            new_scales = work.tile([P, PIECE_COLS], U8, align_bytes=64)
+            new_codes = pieces.tile([P, PIECE_COLS], U32, align_bytes=64)
+            new_scales = pieces.tile([P, PIECE_COLS], U8, align_bytes=64)
             nc.vector.quantize_mx(
                 out=new_codes[:].bitcast(FP8X4),
                 scales=new_scales[:],
@@ -134,8 +134,11 @@ def tile_memory_pb_s_kernel(tc, w, memory, add, out):
             if u + LEAD < N_BANKS:
                 write_bank(u + LEAD)
             add_bank(u)
-            if u == BANKS_PER_PIECE:
-                quantise_w()
-            if u >= BANKS_PER_PIECE and u % BANKS_PER_PIECE == 0:
-                read_piece(u // BANKS_PER_PIECE - 1)
-        read_piece(N_PIECES - 1)
+
+        nc.vector.quantize_mx(
+            out=w_codes[:].bitcast(FP8X4),
+            scales=w_scales[:],
+            in_=w_grouped[:].rearrange("p b t -> p (b t)"),
+        )
+        for i in range(N_PIECES):
+            read_piece(i)

@@ -20,6 +20,7 @@ BANKS_PER_PIECE = PIECE_COLS // BANK_COLS
 N_BANKS = WIDTH // BANK_COLS
 NEW_BANKS = 5
 LEAD = NEW_BANKS - 1
+LOAD_WIDTHS = (256, 256, 512, 512, 512)
 SHARE = 4
 
 FLOPS = 2 * (2 * P * SLOTS * WIDTH)
@@ -42,16 +43,17 @@ def tile_memory_pb_s_kernel(tc, w, memory, add, out):
 
         w_sb = keep.tile([P, SLOTS], BF16)
         nc.sync.dma_start(out=w_sb[:], in_=w)
-        a_tiles = []
-        mem_tiles = []
-        for i in range(N_PIECES):
-            cols = slice(i * PIECE_COLS, (i + 1) * PIECE_COLS)
-            a_sb = pieces.tile([P, PIECE_COLS], BF16)
+        loaded = []
+        first = 0
+        for n, width in enumerate(LOAD_WIDTHS):
+            cols = slice(first, first + width)
+            a_sb = keep.tile([P, width], BF16, name="a_sb%d" % n)
             nc.sync.dma_start(out=a_sb[:], in_=add_rows[:, cols])
-            mem_sb = pieces.tile([P, PACK, PIECE_COLS], BF16)
+            mem_sb = keep.tile([P, PACK, width], BF16, name="mem_sb%d" % n)
             nc.sync.dma_start(out=mem_sb[:], in_=mem_rows[:, :, cols])
-            a_tiles.append(a_sb)
-            mem_tiles.append(mem_sb)
+            for c in range(0, width, BANK_COLS):
+                loaded.append((a_sb, mem_sb, c))
+            first += width
 
         ident = keep.tile([P, P], BF16)
         make_identity(nc, ident[:])
@@ -76,13 +78,13 @@ def tile_memory_pb_s_kernel(tc, w, memory, add, out):
             grouped_tiles.append(new_grouped)
 
         def write_bank(u):
-            i, j = divmod(u, BANKS_PER_PIECE)
+            a_sb, mem_sb, c = loaded[u]
             written = psum_new.tile([P, PACK, BANK_COLS], F32)
             for t in range(PACK):
                 nc.tensor.matmul(
                     written[:, t, :],
                     lhsT=w_by_t[:, t, :],
-                    rhs=a_tiles[i][:, j * BANK_COLS : (j + 1) * BANK_COLS],
+                    rhs=a_sb[:, c : c + BANK_COLS],
                     start=True,
                     stop=True,
                 )
@@ -92,7 +94,8 @@ def tile_memory_pb_s_kernel(tc, w, memory, add, out):
             i, j = divmod(u, BANKS_PER_PIECE)
             cols = slice(j * BANK_COLS, (j + 1) * BANK_COLS)
             written_by_col = written_banks[u][:].rearrange("p t d -> p d t")
-            mem_by_col = mem_tiles[i][:, :, cols].rearrange("p t d -> p d t")
+            a_sb, mem_sb, c = loaded[u]
+            mem_by_col = mem_sb[:, :, c : c + BANK_COLS].rearrange("p t d -> p d t")
             if u % SHARE == 1:
                 staged = stage.tile([P, BANK_COLS, PACK], F32)
                 nc.scalar.copy(out=staged[:], in_=written_by_col)

@@ -21,7 +21,8 @@ N_BANKS = WIDTH // BANK_COLS
 NEW_BANKS = 5
 LEAD = NEW_BANKS - 1
 LOAD_WIDTHS = (256, 256, 512, 512, 512)
-SHARE = 4
+ADDER = "VGVGVVGVVGVVVVVT"
+W_TURN = 8
 
 FLOPS = 2 * (2 * P * SLOTS * WIDTH)
 
@@ -36,7 +37,7 @@ def tile_memory_pb_s_kernel(tc, w, memory, add, out):
         ctx.enter_context(tc.manual_schedule())
         keep = ctx.enter_context(tc.tile_pool(name="keep", bufs=1))
         pieces = ctx.enter_context(tc.tile_pool(name="pieces", bufs=N_PIECES))
-        stage = ctx.enter_context(tc.tile_pool(name="stage", bufs=N_BANKS // SHARE))
+        stage = ctx.enter_context(tc.tile_pool(name="stage", bufs=len([x for x in ADDER if x == "G"])))
         psum_w = ctx.enter_context(tc.psum_pool(name="psum_w", bufs=1))
         psum_new = ctx.enter_context(tc.psum_pool(name="psum_new", bufs=NEW_BANKS))
         psum_out = ctx.enter_context(tc.psum_pool(name="psum_out", bufs=2))
@@ -80,14 +81,23 @@ def tile_memory_pb_s_kernel(tc, w, memory, add, out):
         def write_bank(u):
             a_sb, mem_sb, c = loaded[u]
             written = psum_new.tile([P, PACK, BANK_COLS], F32)
+            by_tensor = ADDER[u] == "T"
             for t in range(PACK):
                 nc.tensor.matmul(
                     written[:, t, :],
                     lhsT=w_by_t[:, t, :],
                     rhs=a_sb[:, c : c + BANK_COLS],
                     start=True,
-                    stop=True,
+                    stop=not by_tensor,
                 )
+                if by_tensor:
+                    nc.tensor.matmul(
+                        written[:, t, :],
+                        lhsT=ident[:],
+                        rhs=mem_sb[:, t, c : c + BANK_COLS],
+                        start=False,
+                        stop=True,
+                    )
             written_banks[u] = written
 
         def add_bank(u):
@@ -96,7 +106,9 @@ def tile_memory_pb_s_kernel(tc, w, memory, add, out):
             written_by_col = written_banks[u][:].rearrange("p t d -> p d t")
             a_sb, mem_sb, c = loaded[u]
             mem_by_col = mem_sb[:, :, c : c + BANK_COLS].rearrange("p t d -> p d t")
-            if u % SHARE == 1:
+            if ADDER[u] == "T":
+                nc.scalar.copy(out=grouped_tiles[i][:, cols, :], in_=written_by_col)
+            elif ADDER[u] == "G":
                 staged = stage.tile([P, BANK_COLS, PACK], F32)
                 nc.scalar.copy(out=staged[:], in_=written_by_col)
                 nc.gpsimd.tensor_tensor(
@@ -131,12 +143,12 @@ def tile_memory_pb_s_kernel(tc, w, memory, add, out):
 
         for u in range(LEAD):
             write_bank(u)
-            if u == BANKS_PER_PIECE - 1:
-                transpose_w()
         for u in range(N_BANKS):
             if u + LEAD < N_BANKS:
                 write_bank(u + LEAD)
             add_bank(u)
+            if u == W_TURN:
+                transpose_w()
 
         nc.vector.quantize_mx(
             out=w_codes[:].bitcast(FP8X4),

@@ -18,8 +18,9 @@ PIECE_COLS = 256
 N_PIECES = WIDTH // PIECE_COLS
 BANKS_PER_PIECE = PIECE_COLS // BANK_COLS
 N_BANKS = WIDTH // BANK_COLS
-NEW_BANKS = 5
-LEAD = NEW_BANKS - 1
+EARLY_SLOTS = 5
+LATE_SLOTS = 3
+FIRST_LATE = 10
 LOAD_WIDTHS = (256, 256, 512, 512, 512)
 ADDER = "VGVGVVGVVGVVVVVT"
 W_TURN = 8
@@ -38,9 +39,8 @@ def tile_memory_pb_s_kernel(tc, w, memory, add, out):
         keep = ctx.enter_context(tc.tile_pool(name="keep", bufs=1))
         pieces = ctx.enter_context(tc.tile_pool(name="pieces", bufs=N_PIECES))
         stage = ctx.enter_context(tc.tile_pool(name="stage", bufs=len([x for x in ADDER if x == "G"])))
-        psum_w = ctx.enter_context(tc.psum_pool(name="psum_w", bufs=1))
-        psum_new = ctx.enter_context(tc.psum_pool(name="psum_new", bufs=NEW_BANKS))
-        psum_out = ctx.enter_context(tc.psum_pool(name="psum_out", bufs=2))
+        psum_early = ctx.enter_context(tc.psum_pool(name="psum_early", bufs=EARLY_SLOTS))
+        psum_late = ctx.enter_context(tc.psum_pool(name="psum_late", bufs=LATE_SLOTS))
 
         w_sb = keep.tile([P, SLOTS], BF16)
         nc.sync.dma_start(out=w_sb[:], in_=w)
@@ -67,7 +67,7 @@ def tile_memory_pb_s_kernel(tc, w, memory, add, out):
         w_scales = keep.tile([P, P], U8, align_bytes=64)
 
         def transpose_w():
-            wT_ps = psum_w.tile([P, PACK, P], BF16)
+            wT_ps = psum_early.tile([P, PACK, P], BF16, tag="early")
             for t in range(PACK):
                 nc.tensor.transpose(wT_ps[:, t, :], w_by_t[:, t, :], ident[:])
             nc.scalar.copy(out=w_grouped[:], in_=wT_ps[:].rearrange("p t b -> p b t"))
@@ -80,7 +80,10 @@ def tile_memory_pb_s_kernel(tc, w, memory, add, out):
 
         def write_bank(u):
             a_sb, mem_sb, c = loaded[u]
-            written = psum_new.tile([P, PACK, BANK_COLS], F32)
+            if u < FIRST_LATE:
+                written = psum_early.tile([P, PACK, BANK_COLS], F32, tag="early")
+            else:
+                written = psum_late.tile([P, PACK, BANK_COLS], F32, tag="late")
             by_tensor = ADDER[u] == "T"
             for t in range(PACK):
                 nc.tensor.matmul(
@@ -127,7 +130,7 @@ def tile_memory_pb_s_kernel(tc, w, memory, add, out):
                 scales=new_scales[:],
                 in_=grouped_tiles[i][:].rearrange("p d t -> p (d t)"),
             )
-            read = psum_out.tile([P, PIECE_COLS], F32)
+            read = psum_early.tile([P, PIECE_COLS], F32, tag="early")
             nc.tensor.matmul_mx(
                 out=read[:],
                 lhsT=w_codes[:].bitcast(FP8X4),
@@ -141,11 +144,15 @@ def tile_memory_pb_s_kernel(tc, w, memory, add, out):
             nc.scalar.copy(out=result[:], in_=read[:])
             nc.sync.dma_start(out=out_rows[:, i * PIECE_COLS : (i + 1) * PIECE_COLS], in_=result[:])
 
-        for u in range(LEAD):
-            write_bank(u)
+        def written_before(x):
+            if x < FIRST_LATE:
+                return max(0, x - EARLY_SLOTS + 1)
+            return max(FIRST_LATE - EARLY_SLOTS, x - LATE_SLOTS + 1)
+
         for u in range(N_BANKS):
-            if u + LEAD < N_BANKS:
-                write_bank(u + LEAD)
+            for x in range(N_BANKS):
+                if written_before(x) == u:
+                    write_bank(x)
             add_bank(u)
             if u == W_TURN:
                 transpose_w()

@@ -13,16 +13,14 @@ P = 128
 PACK = 4
 SLOTS = P * PACK
 WIDTH = 2048
-BANK_COLS = 128
-PIECE_COLS = 256
-N_PIECES = WIDTH // PIECE_COLS
-BANKS_PER_PIECE = PIECE_COLS // BANK_COLS
-N_BANKS = WIDTH // BANK_COLS
+UNIT = 64
+LOAD_WIDTHS = (256, 256, 256, 256, 512, 512)
+SPANS = ((128, "V"), (128, "G"), (128, "V"), (128, "G"), (128, "V"), (128, "V"), (128, "G"), (128, "V"), (128, "V"), (128, "G"), (128, "V"), (128, "V"), (128, "V"), (128, "V"), (128, "V"), (128, "T"))
+QUANT_COLS = (256, 256, 256, 256, 256, 256, 256, 256)
+PASS_COLS = 256
 EARLY_SLOTS = 5
 LATE_SLOTS = 3
 FIRST_LATE = 10
-LOAD_WIDTHS = (256, 256, 512, 512, 512)
-ADDER = "VGVGVVGVVGVVVVVT"
 W_TURN = 8
 
 FLOPS = 2 * (2 * P * SLOTS * WIDTH)
@@ -30,15 +28,16 @@ FLOPS = 2 * (2 * P * SLOTS * WIDTH)
 
 def tile_memory_pb_s_kernel(tc, w, memory, add, out):
     nc = tc.nc
-    mem_rows = memory.rearrange("(p t) c h w -> p t (c h w)", t=PACK)
+    mem_rows = memory.rearrange("(t p) c h w -> p t (c h w)", t=PACK)
     add_rows = add.rearrange("b c h w -> b (c h w)")
     out_rows = out.rearrange("b c h w -> b (c h w)")
+    n_spans = len(SPANS)
 
     with ExitStack() as ctx:
         ctx.enter_context(tc.manual_schedule())
         keep = ctx.enter_context(tc.tile_pool(name="keep", bufs=1))
-        pieces = ctx.enter_context(tc.tile_pool(name="pieces", bufs=N_PIECES))
-        stage = ctx.enter_context(tc.tile_pool(name="stage", bufs=len([x for x in ADDER if x == "G"])))
+        stage = ctx.enter_context(tc.tile_pool(name="stage", bufs=len([s for s in SPANS if s[1] == "G"])))
+        results = ctx.enter_context(tc.tile_pool(name="results", bufs=WIDTH // PASS_COLS))
         psum_early = ctx.enter_context(tc.psum_pool(name="psum_early", bufs=EARLY_SLOTS))
         psum_late = ctx.enter_context(tc.psum_pool(name="psum_late", bufs=LATE_SLOTS))
 
@@ -47,113 +46,99 @@ def tile_memory_pb_s_kernel(tc, w, memory, add, out):
         loaded = []
         first = 0
         for n, width in enumerate(LOAD_WIDTHS):
-            cols = slice(first, first + width)
             a_sb = keep.tile([P, width], BF16, name="a_sb%d" % n)
-            nc.sync.dma_start(out=a_sb[:], in_=add_rows[:, cols])
+            nc.sync.dma_start(out=a_sb[:], in_=add_rows[:, first : first + width])
             mem_sb = keep.tile([P, PACK, width], BF16, name="mem_sb%d" % n)
-            nc.sync.dma_start(out=mem_sb[:], in_=mem_rows[:, :, cols])
-            for c in range(0, width, BANK_COLS):
-                loaded.append((a_sb, mem_sb, c))
+            nc.sync.dma_start(out=mem_sb[:], in_=mem_rows[:, :, first : first + width])
+            loaded.extend([(a_sb, mem_sb, c) for c in range(0, width, UNIT)])
             first += width
 
         ident = keep.tile([P, P], BF16)
         make_identity(nc, ident[:])
 
-        w_by_t = keep.tile([P, PACK, P], BF16)
-        nc.vector.tensor_copy(out=w_by_t[:], in_=w_sb[:].rearrange("b (p t) -> b t p", t=PACK))
+        w_by_t = [w_sb[:, t * P : (t + 1) * P] for t in range(PACK)]
 
         w_grouped = keep.tile([P, P, PACK], BF16, align_bytes=64)
         w_codes = keep.tile([P, P], U32, align_bytes=64)
         w_scales = keep.tile([P, P], U8, align_bytes=64)
+        new_grouped = keep.tile([P, WIDTH, PACK], BF16, align_bytes=64)
+        new_codes = keep.tile([P, WIDTH], U32, align_bytes=64)
+        new_scales = keep.tile([P, WIDTH], U8, align_bytes=64)
 
         def transpose_w():
             wT_ps = psum_early.tile([P, PACK, P], BF16, tag="early")
             for t in range(PACK):
-                nc.tensor.transpose(wT_ps[:, t, :], w_by_t[:, t, :], ident[:])
+                nc.tensor.transpose(wT_ps[:, t, :], w_by_t[t], ident[:])
             nc.scalar.copy(out=w_grouped[:], in_=wT_ps[:].rearrange("p t b -> p b t"))
 
-        written_banks = {}
-        grouped_tiles = []
-        for i in range(N_PIECES):
-            new_grouped = pieces.tile([P, PIECE_COLS, PACK], BF16, align_bytes=64)
-            grouped_tiles.append(new_grouped)
+        starts = [sum([s[0] for s in SPANS[:x]]) for x in range(n_spans)]
+        written_tiles = {}
 
-        def write_bank(u):
-            a_sb, mem_sb, c = loaded[u]
-            if u < FIRST_LATE:
-                written = psum_early.tile([P, PACK, BANK_COLS], F32, tag="early")
+        def write_span(x):
+            width, adder = SPANS[x]
+            a_sb, mem_sb, c = loaded[starts[x] // UNIT]
+            if x < FIRST_LATE:
+                written = psum_early.tile([P, PACK, width], F32, tag="early")
             else:
-                written = psum_late.tile([P, PACK, BANK_COLS], F32, tag="late")
-            by_tensor = ADDER[u] == "T"
+                written = psum_late.tile([P, PACK, width], F32, tag="late")
             for t in range(PACK):
                 nc.tensor.matmul(
-                    written[:, t, :],
-                    lhsT=w_by_t[:, t, :],
-                    rhs=a_sb[:, c : c + BANK_COLS],
-                    start=True,
-                    stop=not by_tensor,
+                    written[:, t, :], lhsT=w_by_t[t], rhs=a_sb[:, c : c + width], start=True, stop=adder != "T"
                 )
-                if by_tensor:
+                if adder == "T":
                     nc.tensor.matmul(
-                        written[:, t, :],
-                        lhsT=ident[:],
-                        rhs=mem_sb[:, t, c : c + BANK_COLS],
-                        start=False,
-                        stop=True,
+                        written[:, t, :], lhsT=ident[:], rhs=mem_sb[:, t, c : c + width], start=False, stop=True
                     )
-            written_banks[u] = written
+            written_tiles[x] = written
 
-        def add_bank(u):
-            i, j = divmod(u, BANKS_PER_PIECE)
-            cols = slice(j * BANK_COLS, (j + 1) * BANK_COLS)
-            written_by_col = written_banks[u][:].rearrange("p t d -> p d t")
-            a_sb, mem_sb, c = loaded[u]
-            mem_by_col = mem_sb[:, :, c : c + BANK_COLS].rearrange("p t d -> p d t")
-            if ADDER[u] == "T":
-                nc.scalar.copy(out=grouped_tiles[i][:, cols, :], in_=written_by_col)
-            elif ADDER[u] == "G":
-                staged = stage.tile([P, BANK_COLS, PACK], F32)
+        def add_span(x):
+            width, adder = SPANS[x]
+            a_sb, mem_sb, c = loaded[starts[x] // UNIT]
+            written_by_col = written_tiles[x][:].rearrange("p t d -> p d t")
+            mem_by_col = mem_sb[:, :, c : c + width].rearrange("p t d -> p d t")
+            new_span = new_grouped[:, starts[x] : starts[x] + width, :]
+            if adder == "T":
+                nc.scalar.copy(out=new_span, in_=written_by_col)
+            elif adder == "G":
+                staged = stage.tile([P, width, PACK], F32, tag="staged")
                 nc.scalar.copy(out=staged[:], in_=written_by_col)
-                nc.gpsimd.tensor_tensor(
-                    out=grouped_tiles[i][:, cols, :], in0=staged[:], in1=mem_by_col, op=mybir.AluOpType.add
-                )
+                nc.gpsimd.tensor_tensor(out=new_span, in0=staged[:], in1=mem_by_col, op=mybir.AluOpType.add)
             else:
-                nc.vector.tensor_tensor(
-                    out=grouped_tiles[i][:, cols, :], in0=written_by_col, in1=mem_by_col, op=mybir.AluOpType.add
-                )
+                nc.vector.tensor_tensor(out=new_span, in0=written_by_col, in1=mem_by_col, op=mybir.AluOpType.add)
 
-        def read_piece(i):
-            new_codes = pieces.tile([P, PIECE_COLS], U32, align_bytes=64)
-            new_scales = pieces.tile([P, PIECE_COLS], U8, align_bytes=64)
+        def quantise(c, width):
             nc.vector.quantize_mx(
-                out=new_codes[:].bitcast(FP8X4),
-                scales=new_scales[:],
-                in_=grouped_tiles[i][:].rearrange("p d t -> p (d t)"),
+                out=new_codes[:, c : c + width].bitcast(FP8X4),
+                scales=new_scales[:, c : c + width],
+                in_=new_grouped[:, c : c + width, :].rearrange("p d t -> p (d t)"),
             )
-            read = psum_early.tile([P, PIECE_COLS], F32, tag="early")
+
+        def read_pass(c):
+            cols = slice(c, c + PASS_COLS)
+            read = psum_early.tile([P, PASS_COLS], F32, tag="early")
             nc.tensor.matmul_mx(
                 out=read[:],
                 lhsT=w_codes[:].bitcast(FP8X4),
                 lhsT_scale=w_scales[:],
-                rhs=new_codes[:].bitcast(FP8X4),
-                rhs_scale=new_scales[:],
+                rhs=new_codes[:, cols].bitcast(FP8X4),
+                rhs_scale=new_scales[:, cols],
                 start=True,
                 stop=True,
             )
-            result = pieces.tile([P, PIECE_COLS], F32)
+            result = results.tile([P, PASS_COLS], F32)
             nc.scalar.copy(out=result[:], in_=read[:])
-            nc.sync.dma_start(out=out_rows[:, i * PIECE_COLS : (i + 1) * PIECE_COLS], in_=result[:])
+            nc.sync.dma_start(out=out_rows[:, cols], in_=result[:])
 
         def written_before(x):
             if x < FIRST_LATE:
                 return max(0, x - EARLY_SLOTS + 1)
             return max(FIRST_LATE - EARLY_SLOTS, x - LATE_SLOTS + 1)
 
-        for u in range(N_BANKS):
-            for x in range(N_BANKS):
+        for u in range(n_spans):
+            for x in range(n_spans):
                 if written_before(x) == u:
-                    write_bank(x)
-            add_bank(u)
+                    write_span(x)
+            add_span(u)
             if u == W_TURN:
                 transpose_w()
 
@@ -162,5 +147,9 @@ def tile_memory_pb_s_kernel(tc, w, memory, add, out):
             scales=w_scales[:],
             in_=w_grouped[:].rearrange("p b t -> p (b t)"),
         )
-        for i in range(N_PIECES):
-            read_piece(i)
+        first = 0
+        for width in QUANT_COLS:
+            quantise(first, width)
+            for c in range(first, first + width, PASS_COLS):
+                read_pass(c)
+            first += width

@@ -14,13 +14,13 @@ PACK = 4
 SLOTS = P * PACK
 WIDTH = 2048
 UNIT = 64
-LOAD_WIDTHS = (256, 256, 256, 256, 512, 512)
-SPANS = ((128, "V"), (128, "G"), (128, "V"), (128, "G"), (128, "V"), (128, "V"), (128, "G"), (128, "V"), (128, "V"), (128, "G"), (128, "V"), (128, "V"), (128, "V"), (128, "V"), (128, "V"), (128, "T"))
+LOAD_WIDTHS = (256, 256, 512, 512, 512)
+SPANS = ((128, "V"), (128, "V"), (128, "G"), (128, "V"), (128, "V"), (128, "G"), (128, "V"), (128, "V"), (128, "G"), (128, "V"), (128, "V"), (64, "G"), (64, "T"), (128, "V"), (128, "V"), (128, "V"), (128, "T"))
 QUANT_COLS = (256, 256, 256, 256, 256, 256, 256, 256)
 PASS_COLS = 256
 EARLY_SLOTS = 5
 LATE_SLOTS = 3
-FIRST_LATE = 10
+FIRST_LATE = 11
 W_TURN = 8
 
 FLOPS = 2 * (2 * P * SLOTS * WIDTH)

@@ -21,6 +21,7 @@ PASS_COLS = 256
 EARLY_SLOTS = 5
 LATE_SLOTS = 3
 FIRST_LATE = 11
+RUN = 4
 W_TURN = 8
 
 FLOPS = 2 * (2 * P * SLOTS * WIDTH)
@@ -104,7 +105,12 @@ def tile_memory_pb_s_kernel(tc, w, memory, add, out):
                 nc.scalar.copy(out=staged[:], in_=written_by_col)
                 nc.gpsimd.tensor_tensor(out=new_span, in0=staged[:], in1=mem_by_col, op=mybir.AluOpType.add)
             else:
-                nc.vector.tensor_tensor(out=new_span, in0=written_by_col, in1=mem_by_col, op=mybir.AluOpType.add)
+                nc.vector.tensor_tensor(
+                    out=new_span.rearrange("p (c i) t -> p c t i", i=RUN),
+                    in0=written_tiles[x][:].rearrange("p t (c i) -> p c t i", i=RUN),
+                    in1=mem_sb[:, :, c : c + width].rearrange("p t (c i) -> p c t i", i=RUN),
+                    op=mybir.AluOpType.add,
+                )
 
         def quantise(c, width):
             nc.vector.quantize_mx(

@@ -15,7 +15,7 @@ SLOTS = P * PACK
 WIDTH = 2048
 UNIT = 64
 LOAD_WIDTHS = (256, 256, 512, 512, 512)
-SPANS = ((128, "V"), (128, "V"), (128, "G"), (128, "V"), (128, "V"), (128, "G"), (128, "V"), (128, "V"), (128, "G"), (128, "V"), (128, "V"), (64, "G"), (64, "T"), (128, "V"), (128, "V"), (128, "V"), (128, "T"))
+SPANS = ((128, "V"), (128, "V"), (128, "V"), (128, "V"), (128, "G"), (128, "V"), (128, "V"), (128, "V"), (128, "G"), (128, "V"), (128, "V"), (128, "G"), (128, "V"), (128, "V"), (64, "V"), (64, "T"), (128, "T"))
 QUANT_COLS = (256, 256, 256, 256, 256, 256, 256, 256)
 PASS_COLS = 256
 EARLY_SLOTS = 5

@@ -14,15 +14,26 @@ PACK = 4
 SLOTS = P * PACK
 WIDTH = 2048
 UNIT = 64
-LOAD_WIDTHS = (256, 256, 512, 512, 512)
+LOADS = (
+    ("w", 0, 512),
+    ("a", 0, 256),
+    ("mem", 0, 256),
+    ("a", 256, 768),
+    ("mem", 256, 256),
+    ("mem", 512, 512),
+    ("a", 1024, 1024),
+    ("mem", 1024, 512),
+    ("mem", 1536, 256),
+    ("mem", 1792, 256),
+)
 SPANS = ((128, "V"), (128, "V"), (128, "V"), (128, "V"), (128, "G"), (128, "V"), (128, "V"), (128, "V"), (128, "G"), (128, "V"), (128, "V"), (128, "G"), (128, "V"), (128, "V"), (64, "V"), (64, "T"), (128, "T"))
-QUANT_COLS = (256, 256, 256, 256, 256, 256, 256, 256)
 PASS_COLS = 256
 EARLY_SLOTS = 5
 LATE_SLOTS = 3
 FIRST_LATE = 11
+EARLY_QUANT = 4
+EARLY_READ = 12
 RUN = 4
-W_TURN = 8
 
 FLOPS = 2 * (2 * P * SLOTS * WIDTH)
 
@@ -43,16 +54,21 @@ def tile_memory_pb_s_kernel(tc, w, memory, add, out):
         psum_late = ctx.enter_context(tc.psum_pool(name="psum_late", bufs=LATE_SLOTS))
 
         w_sb = keep.tile([P, SLOTS], BF16)
-        nc.sync.dma_start(out=w_sb[:], in_=w)
-        loaded = []
-        first = 0
-        for n, width in enumerate(LOAD_WIDTHS):
-            a_sb = keep.tile([P, width], BF16, name="a_sb%d" % n)
-            nc.sync.dma_start(out=a_sb[:], in_=add_rows[:, first : first + width])
-            mem_sb = keep.tile([P, PACK, width], BF16, name="mem_sb%d" % n)
-            nc.sync.dma_start(out=mem_sb[:], in_=mem_rows[:, :, first : first + width])
-            loaded.extend([(a_sb, mem_sb, c) for c in range(0, width, UNIT)])
-            first += width
+        a_at = {}
+        mem_at = {}
+        for tensor, first, width in LOADS:
+            if tensor == "w":
+                nc.sync.dma_start(out=w_sb[:], in_=w)
+            elif tensor == "a":
+                a_sb = keep.tile([P, width], BF16, name="a_sb%d" % first)
+                nc.sync.dma_start(out=a_sb[:], in_=add_rows[:, first : first + width])
+                for c in range(0, width, UNIT):
+                    a_at[first + c] = (a_sb, c)
+            else:
+                mem_sb = keep.tile([P, PACK, width], BF16, name="mem_sb%d" % first)
+                nc.sync.dma_start(out=mem_sb[:], in_=mem_rows[:, :, first : first + width])
+                for c in range(0, width, UNIT):
+                    mem_at[first + c] = (mem_sb, c)
 
         ident = keep.tile([P, P], BF16)
         make_identity(nc, ident[:])
@@ -67,36 +83,45 @@ def tile_memory_pb_s_kernel(tc, w, memory, add, out):
         new_scales = keep.tile([P, WIDTH], U8, align_bytes=64)
 
         def transpose_w():
-            wT_ps = psum_early.tile([P, PACK, P], BF16, tag="early")
+            wT_ps = psum_late.tile([P, PACK, P], BF16, tag="late")
             for t in range(PACK):
                 nc.tensor.transpose(wT_ps[:, t, :], w_by_t[t], ident[:])
+            return wT_ps
+
+        def quantise_w(wT_ps):
             nc.scalar.copy(out=w_grouped[:], in_=wT_ps[:].rearrange("p t b -> p b t"))
+            nc.vector.quantize_mx(
+                out=w_codes[:].bitcast(FP8X4),
+                scales=w_scales[:],
+                in_=w_grouped[:].rearrange("p b t -> p (b t)"),
+            )
 
         starts = [sum([s[0] for s in SPANS[:x]]) for x in range(n_spans)]
         written_tiles = {}
 
         def write_span(x):
             width, adder = SPANS[x]
-            a_sb, mem_sb, c = loaded[starts[x] // UNIT]
+            a_sb, ca = a_at[starts[x]]
+            mem_sb, cm = mem_at[starts[x]]
             if x < FIRST_LATE:
                 written = psum_early.tile([P, PACK, width], F32, tag="early")
             else:
                 written = psum_late.tile([P, PACK, width], F32, tag="late")
             for t in range(PACK):
                 nc.tensor.matmul(
-                    written[:, t, :], lhsT=w_by_t[t], rhs=a_sb[:, c : c + width], start=True, stop=adder != "T"
+                    written[:, t, :], lhsT=w_by_t[t], rhs=a_sb[:, ca : ca + width], start=True, stop=adder != "T"
                 )
                 if adder == "T":
                     nc.tensor.matmul(
-                        written[:, t, :], lhsT=ident[:], rhs=mem_sb[:, t, c : c + width], start=False, stop=True
+                        written[:, t, :], lhsT=ident[:], rhs=mem_sb[:, t, cm : cm + width], start=False, stop=True
                     )
             written_tiles[x] = written
 
         def add_span(x):
             width, adder = SPANS[x]
-            a_sb, mem_sb, c = loaded[starts[x] // UNIT]
+            mem_sb, cm = mem_at[starts[x]]
             written_by_col = written_tiles[x][:].rearrange("p t d -> p d t")
-            mem_by_col = mem_sb[:, :, c : c + width].rearrange("p t d -> p d t")
+            mem_by_col = mem_sb[:, :, cm : cm + width].rearrange("p t d -> p d t")
             new_span = new_grouped[:, starts[x] : starts[x] + width, :]
             if adder == "T":
                 nc.scalar.copy(out=new_span, in_=written_by_col)
@@ -108,7 +133,7 @@ def tile_memory_pb_s_kernel(tc, w, memory, add, out):
                 nc.vector.tensor_tensor(
                     out=new_span.rearrange("p (c i) t -> p c t i", i=RUN),
                     in0=written_tiles[x][:].rearrange("p t (c i) -> p c t i", i=RUN),
-                    in1=mem_sb[:, :, c : c + width].rearrange("p t (c i) -> p c t i", i=RUN),
+                    in1=mem_sb[:, :, cm : cm + width].rearrange("p t (c i) -> p c t i", i=RUN),
                     op=mybir.AluOpType.add,
                 )
 
@@ -135,27 +160,28 @@ def tile_memory_pb_s_kernel(tc, w, memory, add, out):
             nc.scalar.copy(out=result[:], in_=read[:])
             nc.sync.dma_start(out=out_rows[:, cols], in_=result[:])
 
-        def written_before(x):
+        def slot_free(x):
+            if x < EARLY_SLOTS or FIRST_LATE <= x < FIRST_LATE + LATE_SLOTS:
+                return 0
             if x < FIRST_LATE:
-                return max(0, x - EARLY_SLOTS + 1)
-            return max(FIRST_LATE - EARLY_SLOTS, x - LATE_SLOTS + 1)
+                return x - EARLY_SLOTS + 1
+            return x - LATE_SLOTS + 1
 
+        wT_ps = None
+        next_write = 0
         for u in range(n_spans):
-            for x in range(n_spans):
-                if written_before(x) == u:
-                    write_span(x)
+            while next_write < n_spans and slot_free(next_write) <= u:
+                if next_write == EARLY_QUANT:
+                    wT_ps = transpose_w()
+                write_span(next_write)
+                next_write += 1
+            if u == EARLY_QUANT:
+                quantise_w(wT_ps)
+                quantise(0, PASS_COLS)
+            if u == EARLY_READ:
+                read_pass(0)
             add_span(u)
-            if u == W_TURN:
-                transpose_w()
 
-        nc.vector.quantize_mx(
-            out=w_codes[:].bitcast(FP8X4),
-            scales=w_scales[:],
-            in_=w_grouped[:].rearrange("p b t -> p (b t)"),
-        )
-        first = 0
-        for width in QUANT_COLS:
-            quantise(first, width)
-            for c in range(first, first + width, PASS_COLS):
-                read_pass(c)
-            first += width
+        for c in range(PASS_COLS, WIDTH, PASS_COLS):
+            quantise(c, PASS_COLS)
+            read_pass(c)

@@ -13,7 +13,7 @@ P = 128
 PACK = 4
 SLOTS = P * PACK
 WIDTH = 2048
-UNIT = 64
+UNIT = 32
 LOADS = (
     ("w", 0, 512),
     ("a", 0, 256),
@@ -26,13 +26,24 @@ LOADS = (
     ("mem", 1536, 256),
     ("mem", 1792, 256),
 )
-SPANS = ((128, "V"), (128, "V"), (128, "V"), (128, "V"), (128, "G"), (128, "V"), (128, "V"), (128, "V"), (128, "G"), (128, "V"), (128, "V"), (128, "G"), (128, "V"), (128, "V"), (64, "V"), (64, "T"), (128, "T"))
+SPANS = (
+    *((128, "V"),) * 4,
+    (128, "G"),
+    *((128, "V"),) * 3,
+    (128, "G"),
+    *((128, "V"),) * 2,
+    (96, "G"),
+    (32, "V"),
+    *((128, "V"),) * 2,
+    (64, "V"),
+    (64, "T"),
+    (128, "T"),
+)
 PASS_COLS = 256
-EARLY_SLOTS = 5
-LATE_SLOTS = 3
-FIRST_LATE = 11
-EARLY_QUANT = 4
-EARLY_READ = 12
+PSUM_SLOTS = 8
+CHUNK = 512
+FIRST_G = 4
+READ_AT = {11: 0, 12: 256}
 RUN = 4
 
 FLOPS = 2 * (2 * P * SLOTS * WIDTH)
@@ -50,8 +61,7 @@ def tile_memory_pb_s_kernel(tc, w, memory, add, out):
         keep = ctx.enter_context(tc.tile_pool(name="keep", bufs=1))
         stage = ctx.enter_context(tc.tile_pool(name="stage", bufs=len([s for s in SPANS if s[1] == "G"])))
         results = ctx.enter_context(tc.tile_pool(name="results", bufs=WIDTH // PASS_COLS))
-        psum_early = ctx.enter_context(tc.psum_pool(name="psum_early", bufs=EARLY_SLOTS))
-        psum_late = ctx.enter_context(tc.psum_pool(name="psum_late", bufs=LATE_SLOTS))
+        psum = ctx.enter_context(tc.psum_pool(name="psum", bufs=PSUM_SLOTS))
 
         w_sb = keep.tile([P, SLOTS], BF16)
         a_at = {}
@@ -78,12 +88,22 @@ def tile_memory_pb_s_kernel(tc, w, memory, add, out):
         w_grouped = keep.tile([P, P, PACK], BF16, align_bytes=64)
         w_codes = keep.tile([P, P], U32, align_bytes=64)
         w_scales = keep.tile([P, P], U8, align_bytes=64)
-        new_grouped = keep.tile([P, WIDTH, PACK], BF16, align_bytes=64)
+        new_chunks = {}
+
+        def new_columns(first, width):
+            chunk = first // CHUNK
+            if chunk not in new_chunks:
+                new_chunks[chunk] = keep.tile(
+                    [P, CHUNK, PACK], BF16, name="new_grouped", tag="new_grouped%d" % max(chunk, 1), align_bytes=64
+                )
+            c = first - chunk * CHUNK
+            return new_chunks[chunk][:, c : c + width, :]
+
         new_codes = keep.tile([P, WIDTH], U32, align_bytes=64)
         new_scales = keep.tile([P, WIDTH], U8, align_bytes=64)
 
         def transpose_w():
-            wT_ps = psum_late.tile([P, PACK, P], BF16, tag="late")
+            wT_ps = psum.tile([P, PACK, P], BF16, tag="bank")
             for t in range(PACK):
                 nc.tensor.transpose(wT_ps[:, t, :], w_by_t[t], ident[:])
             return wT_ps
@@ -103,10 +123,7 @@ def tile_memory_pb_s_kernel(tc, w, memory, add, out):
             width, adder = SPANS[x]
             a_sb, ca = a_at[starts[x]]
             mem_sb, cm = mem_at[starts[x]]
-            if x < FIRST_LATE:
-                written = psum_early.tile([P, PACK, width], F32, tag="early")
-            else:
-                written = psum_late.tile([P, PACK, width], F32, tag="late")
+            written = psum.tile([P, PACK, width], F32, tag="bank")
             for t in range(PACK):
                 nc.tensor.matmul(
                     written[:, t, :], lhsT=w_by_t[t], rhs=a_sb[:, ca : ca + width], start=True, stop=adder != "T"
@@ -122,7 +139,7 @@ def tile_memory_pb_s_kernel(tc, w, memory, add, out):
             mem_sb, cm = mem_at[starts[x]]
             written_by_col = written_tiles[x][:].rearrange("p t d -> p d t")
             mem_by_col = mem_sb[:, :, cm : cm + width].rearrange("p t d -> p d t")
-            new_span = new_grouped[:, starts[x] : starts[x] + width, :]
+            new_span = new_columns(starts[x], width)
             if adder == "T":
                 nc.scalar.copy(out=new_span, in_=written_by_col)
             elif adder == "G":
@@ -141,12 +158,14 @@ def tile_memory_pb_s_kernel(tc, w, memory, add, out):
             nc.vector.quantize_mx(
                 out=new_codes[:, c : c + width].bitcast(FP8X4),
                 scales=new_scales[:, c : c + width],
-                in_=new_grouped[:, c : c + width, :].rearrange("p d t -> p (d t)"),
+                in_=new_columns(c, width).rearrange("p d t -> p (d t)"),
             )
+
+        reads = {}
 
         def read_pass(c):
             cols = slice(c, c + PASS_COLS)
-            read = psum_early.tile([P, PASS_COLS], F32, tag="early")
+            read = psum.tile([P, PASS_COLS], F32, tag="bank")
             nc.tensor.matmul_mx(
                 out=read[:],
                 lhsT=w_codes[:].bitcast(FP8X4),
@@ -156,32 +175,45 @@ def tile_memory_pb_s_kernel(tc, w, memory, add, out):
                 start=True,
                 stop=True,
             )
+            reads[c] = read
+
+        def store_pass(c):
+            cols = slice(c, c + PASS_COLS)
             result = results.tile([P, PASS_COLS], F32)
-            nc.scalar.copy(out=result[:], in_=read[:])
+            nc.scalar.copy(out=result[:], in_=reads[c][:])
             nc.sync.dma_start(out=out_rows[:, cols], in_=result[:])
 
-        def slot_free(x):
-            if x < EARLY_SLOTS or FIRST_LATE <= x < FIRST_LATE + LATE_SLOTS:
-                return 0
-            if x < FIRST_LATE:
-                return x - EARLY_SLOTS + 1
-            return x - LATE_SLOTS + 1
-
+        steps = []
+        for x in range(n_spans):
+            if x == FIRST_G:
+                steps.append(("w", 0))
+            if x in READ_AT:
+                steps.append(("r", READ_AT[x]))
+            steps.append(("span", x))
+        emptied = set()
+        sent = 0
         wT_ps = None
-        next_write = 0
         for u in range(n_spans):
-            while next_write < n_spans and slot_free(next_write) <= u:
-                if next_write == EARLY_QUANT:
+            while sent < len(steps) and (sent < PSUM_SLOTS or steps[sent - PSUM_SLOTS] in emptied):
+                what, which = steps[sent]
+                if what == "w":
                     wT_ps = transpose_w()
-                write_span(next_write)
-                next_write += 1
-            if u == EARLY_QUANT:
+                elif what == "r":
+                    read_pass(which)
+                else:
+                    write_span(which)
+                sent += 1
+            if u == FIRST_G:
                 quantise_w(wT_ps)
-                quantise(0, PASS_COLS)
-            if u == EARLY_READ:
-                read_pass(0)
+                emptied.add(("w", 0))
+                quantise(0, CHUNK)
+            if u in READ_AT:
+                store_pass(READ_AT[u])
+                emptied.add(("r", READ_AT[u]))
             add_span(u)
+            emptied.add(("span", u))
 
-        for c in range(PASS_COLS, WIDTH, PASS_COLS):
+        for c in range(CHUNK, WIDTH, PASS_COLS):
             quantise(c, PASS_COLS)
             read_pass(c)
+            store_pass(c)

@@ -13,7 +13,7 @@ P = 128
 PACK = 4
 SLOTS = P * PACK
 WIDTH = 2048
-UNIT = 32
+UNIT = 64
 LOADS = (
     ("w", 0, 512),
     ("a", 0, 256),
@@ -32,8 +32,8 @@ SPANS = (
     *((128, "V"),) * 3,
     (128, "G"),
     *((128, "V"),) * 2,
-    (96, "G"),
-    (32, "V"),
+    (64, "G"),
+    (64, "V"),
     *((128, "V"),) * 2,
     (64, "V"),
     (64, "T"),

@@ -13,37 +13,16 @@ P = 128
 PACK = 4
 SLOTS = P * PACK
 WIDTH = 2048
-UNIT = 64
-LOADS = (
-    ("w", 0, 512),
-    ("a", 0, 256),
-    ("mem", 0, 256),
-    ("a", 256, 768),
-    ("mem", 256, 256),
-    ("mem", 512, 512),
-    ("a", 1024, 1024),
-    ("mem", 1024, 512),
-    ("mem", 1536, 256),
-    ("mem", 1792, 256),
-)
-SPANS = (
-    *((128, "V"),) * 4,
-    (128, "G"),
-    *((128, "V"),) * 3,
-    (128, "G"),
-    *((128, "V"),) * 2,
-    (64, "G"),
-    (64, "V"),
-    *((128, "V"),) * 2,
-    (64, "V"),
-    (64, "T"),
-    (128, "T"),
-)
+UNIT = 4
+LOADS = (('w', 0, 512), ('a', 0, 256), ('mem', 0, 256), ('a', 256, 256), ('mem', 256, 256), ('a', 512, 512), ('mem', 512, 512), ('a', 1024, 1024), ('mem', 1024, 512), ('mem', 1536, 256), ('mem', 1792, 256))
+SPANS = ((128, 'V'), (128, 'V'), (128, 'V'), (128, 'V'), (128, 'G'), (128, 'V'), (128, 'V'), (128, 'V'), (128, 'G'), (96, 'G'), (32, 'V'), (128, 'V'), (128, 'V'), (128, 'V'), (128, 'V'), (52, 'V'), (76, 'T'), (128, 'T'))
 PASS_COLS = 256
 PSUM_SLOTS = 8
+LAST_PIECES = (256, 256, 256, 256, 256, 256)
+KEEP_WARM = 0
 CHUNK = 512
 FIRST_G = 4
-READ_AT = {11: 0, 12: 256}
+READ_AT = {12: 0, 13: 256}
 RUN = 4
 
 FLOPS = 2 * (2 * P * SLOTS * WIDTH)
@@ -59,8 +38,7 @@ def tile_memory_pb_s_kernel(tc, w, memory, add, out):
     with ExitStack() as ctx:
         ctx.enter_context(tc.manual_schedule())
         keep = ctx.enter_context(tc.tile_pool(name="keep", bufs=1))
-        stage = ctx.enter_context(tc.tile_pool(name="stage", bufs=len([s for s in SPANS if s[1] == "G"])))
-        results = ctx.enter_context(tc.tile_pool(name="results", bufs=WIDTH // PASS_COLS))
+        stage = ctx.enter_context(tc.tile_pool(name="stage", bufs=1))
         psum = ctx.enter_context(tc.psum_pool(name="psum", bufs=PSUM_SLOTS))
 
         w_sb = keep.tile([P, SLOTS], BF16)
@@ -118,6 +96,7 @@ def tile_memory_pb_s_kernel(tc, w, memory, add, out):
 
         starts = [sum([s[0] for s in SPANS[:x]]) for x in range(n_spans)]
         written_tiles = {}
+        staged_at = {}
 
         def write_span(x):
             width, adder = SPANS[x]
@@ -143,9 +122,25 @@ def tile_memory_pb_s_kernel(tc, w, memory, add, out):
             if adder == "T":
                 nc.scalar.copy(out=new_span, in_=written_by_col)
             elif adder == "G":
-                staged = stage.tile([P, width, PACK], F32, tag="staged")
-                nc.scalar.copy(out=staged[:], in_=written_by_col)
-                nc.gpsimd.tensor_tensor(out=new_span, in0=staged[:], in1=mem_by_col, op=mybir.AluOpType.add)
+                joined = [x]
+                while SPANS[joined[0] - 1][1] == "G":
+                    joined.insert(0, joined[0] - 1)
+                while SPANS[joined[-1] + 1][1] == "G":
+                    joined.append(joined[-1] + 1)
+                total = sum([SPANS[y][0] for y in joined])
+                if x == joined[0]:
+                    staged_at[x] = stage.tile([P, total, PACK], F32, name="staged%d" % x)
+                staged = staged_at[joined[0]]
+                c = starts[x] - starts[joined[0]]
+                nc.scalar.copy(out=staged[:, c : c + width, :], in_=written_by_col)
+                if x == joined[-1]:
+                    mem_sb, cm = mem_at[starts[joined[0]]]
+                    nc.gpsimd.tensor_tensor(
+                        out=new_columns(starts[joined[0]], total),
+                        in0=staged[:],
+                        in1=mem_sb[:, :, cm : cm + total].rearrange("p t d -> p d t"),
+                        op=mybir.AluOpType.add,
+                    )
             else:
                 nc.vector.tensor_tensor(
                     out=new_span.rearrange("p (c i) t -> p c t i", i=RUN),
@@ -163,9 +158,8 @@ def tile_memory_pb_s_kernel(tc, w, memory, add, out):
 
         reads = {}
 
-        def read_pass(c):
-            cols = slice(c, c + PASS_COLS)
-            read = psum.tile([P, PASS_COLS], F32, tag="bank")
+        def read_into(read, c, width):
+            cols = slice(c, c + width)
             nc.tensor.matmul_mx(
                 out=read[:],
                 lhsT=w_codes[:].bitcast(FP8X4),
@@ -175,13 +169,17 @@ def tile_memory_pb_s_kernel(tc, w, memory, add, out):
                 start=True,
                 stop=True,
             )
+
+        def read_pass(c, width):
+            read = psum.tile([P, width], F32, tag="bank")
+            read_into(read, c, width)
             reads[c] = read
 
-        def store_pass(c):
-            cols = slice(c, c + PASS_COLS)
-            result = results.tile([P, PASS_COLS], F32)
+        def store_pass(c, width):
+            result = keep.tile([P, width], F32, name="result%d" % c)
             nc.scalar.copy(out=result[:], in_=reads[c][:])
-            nc.sync.dma_start(out=out_rows[:, cols], in_=result[:])
+            queue = nc.scalar if c + width == WIDTH else nc.sync
+            queue.dma_start(out=out_rows[:, c : c + width], in_=result[:])
 
         steps = []
         for x in range(n_spans):
@@ -199,7 +197,7 @@ def tile_memory_pb_s_kernel(tc, w, memory, add, out):
                 if what == "w":
                     wT_ps = transpose_w()
                 elif what == "r":
-                    read_pass(which)
+                    read_pass(which, PASS_COLS)
                 else:
                     write_span(which)
                 sent += 1
@@ -208,12 +206,17 @@ def tile_memory_pb_s_kernel(tc, w, memory, add, out):
                 emptied.add(("w", 0))
                 quantise(0, CHUNK)
             if u in READ_AT:
-                store_pass(READ_AT[u])
+                store_pass(READ_AT[u], PASS_COLS)
                 emptied.add(("r", READ_AT[u]))
             add_span(u)
             emptied.add(("span", u))
 
-        for c in range(CHUNK, WIDTH, PASS_COLS):
-            quantise(c, PASS_COLS)
-            read_pass(c)
-            store_pass(c)
+        again = psum.tile([P, PASS_COLS], F32, tag="bank")
+        for i in range(KEEP_WARM):
+            read_into(again, 0, PASS_COLS)
+        c = CHUNK
+        for width in LAST_PIECES:
+            quantise(c, width)
+            read_pass(c, width)
+            store_pass(c, width)
+            c += width

from contextlib import ExitStack

import concourse.mybir as mybir
from concourse.masks import make_identity

BF16 = mybir.dt.bfloat16
F32 = mybir.dt.float32
U32 = mybir.dt.uint32
U8 = mybir.dt.uint8
FP8X4 = mybir.dt.float8_e4m3fn_x4

P = 128
PACK = 4
SLOTS = P * PACK
WIDTH = 2048
UNIT = 4
LOADS = (('w', 0, 512), ('a', 0, 256), ('mem', 0, 256), ('a', 256, 256), ('mem', 256, 256), ('a', 512, 512), ('mem', 512, 512), ('a', 1024, 1024), ('mem', 1024, 512), ('mem', 1536, 256), ('mem', 1792, 256))
SPANS = ((128, 'V'), (128, 'V'), (128, 'V'), (128, 'V'), (128, 'G'), (128, 'V'), (128, 'V'), (128, 'V'), (128, 'G'), (96, 'G'), (32, 'V'), (128, 'V'), (128, 'V'), (128, 'V'), (128, 'V'), (52, 'V'), (76, 'T'), (128, 'T'))
PASS_COLS = 256
PSUM_SLOTS = 8
LAST_PIECES = (256, 256, 256, 256, 256, 256)
KEEP_WARM = 0
CHUNK = 512
FIRST_G = 4
READ_AT = {12: 0, 13: 256}
RUN = 4

FLOPS = 2 * (2 * P * SLOTS * WIDTH)


def tile_memory_pb_s_kernel(tc, w, memory, add, out):
    nc = tc.nc
    mem_rows = memory.rearrange("(t p) c h w -> p t (c h w)", t=PACK)
    add_rows = add.rearrange("b c h w -> b (c h w)")
    out_rows = out.rearrange("b c h w -> b (c h w)")
    n_spans = len(SPANS)

    with ExitStack() as ctx:
        ctx.enter_context(tc.manual_schedule())
        keep = ctx.enter_context(tc.tile_pool(name="keep", bufs=1))
        stage = ctx.enter_context(tc.tile_pool(name="stage", bufs=1))
        psum = ctx.enter_context(tc.psum_pool(name="psum", bufs=PSUM_SLOTS))

        w_sb = keep.tile([P, SLOTS], BF16)
        a_at = {}
        mem_at = {}
        for tensor, first, width in LOADS:
            if tensor == "w":
                nc.sync.dma_start(out=w_sb[:], in_=w)
            elif tensor == "a":
                a_sb = keep.tile([P, width], BF16, name="a_sb%d" % first)
                nc.sync.dma_start(out=a_sb[:], in_=add_rows[:, first : first + width])
                for c in range(0, width, UNIT):
                    a_at[first + c] = (a_sb, c)
            else:
                mem_sb = keep.tile([P, PACK, width], BF16, name="mem_sb%d" % first)
                nc.sync.dma_start(out=mem_sb[:], in_=mem_rows[:, :, first : first + width])
                for c in range(0, width, UNIT):
                    mem_at[first + c] = (mem_sb, c)

        ident = keep.tile([P, P], BF16)
        make_identity(nc, ident[:])

        w_by_t = [w_sb[:, t * P : (t + 1) * P] for t in range(PACK)]

        w_grouped = keep.tile([P, P, PACK], BF16, align_bytes=64)
        w_codes = keep.tile([P, P], U32, align_bytes=64)
        w_scales = keep.tile([P, P], U8, align_bytes=64)
        new_chunks = {}

        def new_columns(first, width):
            chunk = first // CHUNK
            if chunk not in new_chunks:
                new_chunks[chunk] = keep.tile(
                    [P, CHUNK, PACK], BF16, name="new_grouped", tag="new_grouped%d" % max(chunk, 1), align_bytes=64
                )
            c = first - chunk * CHUNK
            return new_chunks[chunk][:, c : c + width, :]

        new_codes = keep.tile([P, WIDTH], U32, align_bytes=64)
        new_scales = keep.tile([P, WIDTH], U8, align_bytes=64)

        def transpose_w():
            wT_ps = psum.tile([P, PACK, P], BF16, tag="bank")
            for t in range(PACK):
                nc.tensor.transpose(wT_ps[:, t, :], w_by_t[t], ident[:])
            return wT_ps

        def quantise_w(wT_ps):
            nc.scalar.copy(out=w_grouped[:], in_=wT_ps[:].rearrange("p t b -> p b t"))
            nc.vector.quantize_mx(
                out=w_codes[:].bitcast(FP8X4),
                scales=w_scales[:],
                in_=w_grouped[:].rearrange("p b t -> p (b t)"),
            )

        starts = [sum([s[0] for s in SPANS[:x]]) for x in range(n_spans)]
        written_tiles = {}
        staged_at = {}

        def write_span(x):
            width, adder = SPANS[x]
            a_sb, ca = a_at[starts[x]]
            mem_sb, cm = mem_at[starts[x]]
            written = psum.tile([P, PACK, width], F32, tag="bank")
            for t in range(PACK):
                nc.tensor.matmul(
                    written[:, t, :], lhsT=w_by_t[t], rhs=a_sb[:, ca : ca + width], start=True, stop=adder != "T"
                )
                if adder == "T":
                    nc.tensor.matmul(
                        written[:, t, :], lhsT=ident[:], rhs=mem_sb[:, t, cm : cm + width], start=False, stop=True
                    )
            written_tiles[x] = written

        def add_span(x):
            width, adder = SPANS[x]
            mem_sb, cm = mem_at[starts[x]]
            written_by_col = written_tiles[x][:].rearrange("p t d -> p d t")
            mem_by_col = mem_sb[:, :, cm : cm + width].rearrange("p t d -> p d t")
            new_span = new_columns(starts[x], width)
            if adder == "T":
                nc.scalar.copy(out=new_span, in_=written_by_col)
            elif adder == "G":
                joined = [x]
                while SPANS[joined[0] - 1][1] == "G":
                    joined.insert(0, joined[0] - 1)
                while SPANS[joined[-1] + 1][1] == "G":
                    joined.append(joined[-1] + 1)
                total = sum([SPANS[y][0] for y in joined])
                if x == joined[0]:
                    staged_at[x] = stage.tile([P, total, PACK], F32, name="staged%d" % x)
                staged = staged_at[joined[0]]
                c = starts[x] - starts[joined[0]]
                nc.scalar.copy(out=staged[:, c : c + width, :], in_=written_by_col)
                if x == joined[-1]:
                    mem_sb, cm = mem_at[starts[joined[0]]]
                    nc.gpsimd.tensor_tensor(
                        out=new_columns(starts[joined[0]], total),
                        in0=staged[:],
                        in1=mem_sb[:, :, cm : cm + total].rearrange("p t d -> p d t"),
                        op=mybir.AluOpType.add,
                    )
            else:
                nc.vector.tensor_tensor(
                    out=new_span.rearrange("p (c i) t -> p c t i", i=RUN),
                    in0=written_tiles[x][:].rearrange("p t (c i) -> p c t i", i=RUN),
                    in1=mem_sb[:, :, cm : cm + width].rearrange("p t (c i) -> p c t i", i=RUN),
                    op=mybir.AluOpType.add,
                )

        def quantise(c, width):
            nc.vector.quantize_mx(
                out=new_codes[:, c : c + width].bitcast(FP8X4),
                scales=new_scales[:, c : c + width],
                in_=new_columns(c, width).rearrange("p d t -> p (d t)"),
            )

        reads = {}

        def read_into(read, c, width):
            cols = slice(c, c + width)
            nc.tensor.matmul_mx(
                out=read[:],
                lhsT=w_codes[:].bitcast(FP8X4),
                lhsT_scale=w_scales[:],
                rhs=new_codes[:, cols].bitcast(FP8X4),
                rhs_scale=new_scales[:, cols],
                start=True,
                stop=True,
            )

        def read_pass(c, width):
            read = psum.tile([P, width], F32, tag="bank")
            read_into(read, c, width)
            reads[c] = read

        def store_pass(c, width):
            result = keep.tile([P, width], F32, name="result%d" % c)
            nc.scalar.copy(out=result[:], in_=reads[c][:])
            queue = nc.scalar if c + width == WIDTH else nc.sync
            queue.dma_start(out=out_rows[:, c : c + width], in_=result[:])

        steps = []
        for x in range(n_spans):
            if x == FIRST_G:
                steps.append(("w", 0))
            if x in READ_AT:
                steps.append(("r", READ_AT[x]))
            steps.append(("span", x))
        emptied = set()
        sent = 0
        wT_ps = None
        for u in range(n_spans):
            while sent < len(steps) and (sent < PSUM_SLOTS or steps[sent - PSUM_SLOTS] in emptied):
                what, which = steps[sent]
                if what == "w":
                    wT_ps = transpose_w()
                elif what == "r":
                    read_pass(which, PASS_COLS)
                else:
                    write_span(which)
                sent += 1
            if u == FIRST_G:
                quantise_w(wT_ps)
                emptied.add(("w", 0))
                quantise(0, CHUNK)
            if u in READ_AT:
                store_pass(READ_AT[u], PASS_COLS)
                emptied.add(("r", READ_AT[u]))
            add_span(u)
            emptied.add(("span", u))

        again = psum.tile([P, PASS_COLS], F32, tag="bank")
        for i in range(KEEP_WARM):
            read_into(again, 0, PASS_COLS)
        c = CHUNK
        for width in LAST_PIECES:
            quantise(c, width)
            read_pass(c, width)
            store_pass(c, width)
            c += width
